import numpy as np
import ml_dtypes


def mxq(x, axis, fmt="e4m3"):
    dtype, down = {"e4m3": (ml_dtypes.float8_e4m3fn, 7), "e5m2": (ml_dtypes.float8_e5m2, 14)}[fmt]
    v = np.moveaxis(np.asarray(x, np.float32).astype(ml_dtypes.bfloat16).astype(np.float64), axis, -1)
    blocks = v.reshape(v.shape[:-1] + (-1, 32))
    amax = np.abs(blocks).max(-1, keepdims=True)
    byte = np.maximum(np.where(amax > 0, np.frexp(amax)[1] - 1 + 127, 0) - down, 1)
    scale = np.exp2(byte - 127.0)
    codes = (blocks / scale).astype(np.float32).astype(dtype).astype(np.float64)
    return np.moveaxis((codes * scale).reshape(v.shape), -1, axis)


WIDE = False


def mx_kscale(k):
    if not WIDE:
        return np.ones(k)
    levels = np.array([20, -20, 10, -10, 0])
    a = np.random.permutation(np.resize(levels, k // 512 * 4)).reshape(k // 512, 4)
    idx = np.arange(k)
    return np.exp2(a[idx // 512, idx % 128 // 32])


BF16 = ml_dtypes.bfloat16


def bf(x):
    return np.asarray(x, np.float32).astype(BF16)


def f64(x):
    return np.asarray(x).astype(np.float64)


B, P, D = 2048, 2, 512
IN = P * D


def sigmoid(v):
    return 1.0 / (1.0 + np.exp(-v))


def pre_activation(x, weights, bias, gain, norm_bias):
    xn = f64(x) * f64(gain) + f64(norm_bias)
    yp = xn.reshape(B, P, D).transpose(1, 0, 2) @ f64(weights)
    return yp.transpose(1, 0, 2).reshape(B, IN) + f64(bias)


def setup_inputs():
    s = mx_kscale(D)
    sf = np.tile(s, P)
    x = bf(np.random.standard_normal((B, IN)))
    w0 = bf(np.random.standard_normal((P, D, D)) / np.sqrt(D))
    bias = bf(np.random.standard_normal(IN) * 0.3)
    gain = bf(1.3 + 0.1 * np.random.standard_normal(1))
    norm_bias = bf(0.3 + 0.05 * np.random.standard_normal(1))
    gamma = bf(0.5 + 0.3 * np.random.standard_normal(IN))
    beta = bf(np.random.standard_normal(IN))
    g = bf(np.random.standard_normal((B, IN)) * np.exp2(np.random.randint(-12, 1, (B, 1))) * 4.0 * sf)
    y = pre_activation(x, w0, bias, gain, norm_bias)
    weights = bf(f64(w0) * s[None, :, None] / s[None, None, :])
    return {"x": x, "weights": weights, "bias": bias, "gain": gain, "norm_bias": norm_bias,
            "gamma": gamma, "beta": beta, "y": np.asarray(y, np.float32), "grad_out": g}


def reference(x, weights, bias, gain, norm_bias, gamma, beta, y, grad_out):
    g, yf, ga, be = f64(grad_out), f64(y), f64(gamma), f64(beta)
    sg = sigmoid(be * yf)
    dy = g * (ga + (1.0 - ga) * sg * (1.0 + be * yf * (1.0 - sg)))
    dyp = dy.reshape(B, P, D).transpose(1, 0, 2)
    dxp = mxq(dyp, 2, "e5m2") @ mxq(f64(weights), 2, "e4m3").transpose(0, 2, 1)
    return dxp.transpose(1, 0, 2).reshape(B, IN) * f64(gain) + g

@@ -1,0 +1,205 @@
+from contextlib import ExitStack
+
+import concourse.mybir as mybir
+from concourse.masks import make_identity
+
+F32 = mybir.dt.float32
+BF16 = mybir.dt.bfloat16
+U32 = mybir.dt.uint32
+U8 = mybir.dt.uint8
+E4M3_X4 = mybir.dt.float8_e4m3fn_x4
+E5M2_X4 = mybir.dt.float8_e5m2_x4
+ACT = mybir.ActivationFunctionType
+ALU = mybir.AluOpType
+
+P = 128
+PACK = 4
+TOKENS = 2048
+PARTS = 2
+PART = P * PACK
+FEATURES = PARTS * PART
+BLOCKS = FEATURES // P
+TILES = TOKENS // P
+GROUP = 4
+GROUPS = TILES // GROUP
+GROUP_TOKENS = GROUP * P
+HALF_TOKENS = GROUP_TOKENS // 2
+
+FLOPS = 2 * TOKENS * PART * PART * PARTS
+BYTES = TOKENS * FEATURES * (4 + 2 + 4) + PARTS * PART * PART * 2 + 2 * FEATURES * 2 + 2
+
+
+def tile_better_transformer_t_v_kernel(
+    tc, x, weights, bias, gain, norm_bias, gamma, beta, y, grad_out, out
+):
+    nc = tc.nc
+
+    y_view = y.rearrange("(p j) f -> p j f", j=TILES)
+    g_view = grad_out.rearrange("(p j) f -> p j f", j=TILES)
+    out_view = out.rearrange("(p j) f -> p j f", j=TILES)
+
+    with ExitStack() as ctx:
+        keep = ctx.enter_context(tc.tile_pool(name="keep", bufs=1))
+        work = ctx.enter_context(tc.tile_pool(name="work", bufs=2))
+        psum_y = ctx.enter_context(tc.psum_pool(name="psum_y", bufs=4))
+        psum_g = ctx.enter_context(tc.psum_pool(name="psum_g", bufs=2))
+        psum_dx = ctx.enter_context(tc.psum_pool(name="psum_dx", bufs=2))
+
+        vec_rows = keep.tile([P, P], BF16)
+        nc.vector.memset(vec_rows[:], 0.0)
+        nc.sync.dma_start(out=vec_rows[0:BLOCKS, :], in_=gamma.rearrange("(r c) -> r c", c=P))
+        nc.sync.dma_start(out=vec_rows[BLOCKS : 2 * BLOCKS, :], in_=beta.rearrange("(r c) -> r c", c=P))
+        gain_bf = keep.tile([P, 1], BF16)
+        nc.scalar.dma_start(out=gain_bf[:], in_=gain.partition_broadcast(P))
+
+        w_rows = keep.tile([P, PARTS * PACK, PART], BF16)
+        y_rows = {}
+        g_rows = {}
+        for c in range(GROUPS):
+            tiles = slice(c * GROUP, (c + 1) * GROUP)
+            for q in range(PARTS):
+                y_rows[c, q] = keep.tile([P, GROUP, PART], F32, name="y_rows_%d_%d" % (c, q))
+                nc.sync.dma_start(out=y_rows[c, q][:], in_=y_view[:, tiles, q * PART : (q + 1) * PART])
+                if q == 0:
+                    g_rows[c] = keep.tile([P, GROUP, FEATURES], BF16, name="g_rows_%d" % c)
+                    nc.sync.dma_start(out=g_rows[c][:], in_=g_view[:, tiles, :])
+                    if c == 0:
+                        nc.sync.dma_start(
+                            out=w_rows[:], in_=weights.rearrange("q (a p) o -> p (q a) o", p=P)
+                        )
+
+        ident_f32 = keep.tile([P, P], F32)
+        make_identity(nc, ident_f32[:])
+        ident_bf = keep.tile([P, P], BF16)
+        make_identity(nc, ident_bf[:])
+
+        vec_cols = psum_g.tile([P, PACK, HALF_TOKENS], BF16, tag="turned_bf")
+        nc.tensor.transpose(vec_cols[:, 0, 0:P], vec_rows[:], ident_bf[:])
+        gamma_col = keep.tile([P, BLOCKS], F32)
+        nc.vector.tensor_copy(out=gamma_col[:], in_=vec_cols[:, 0, 0:BLOCKS])
+        c_col = keep.tile([P, BLOCKS], F32)
+        nc.vector.tensor_scalar(
+            out=c_col[:], in0=vec_cols[:, 0, 0:BLOCKS], scalar1=1.0, scalar2=0.5, op0=ALU.subtract, op1=ALU.mult
+        )
+        neg_beta_col = keep.tile([P, BLOCKS], F32)
+        nc.vector.tensor_scalar(
+            out=neg_beta_col[:], in0=vec_cols[:, 0, BLOCKS : 2 * BLOCKS], scalar1=-1.0, scalar2=None, op0=ALU.mult
+        )
+        half_beta_col = keep.tile([P, BLOCKS], F32)
+        nc.vector.tensor_scalar(
+            out=half_beta_col[:], in0=vec_cols[:, 0, BLOCKS : 2 * BLOCKS], scalar1=0.5, scalar2=None, op0=ALU.mult
+        )
+        gain_col = keep.tile([P, 1], F32)
+        nc.vector.tensor_copy(out=gain_col[:], in_=gain_bf[:])
+
+        w_grouped = keep.tile([P, PARTS, PART, PACK], BF16, align_bytes=64)
+        w_codes = keep.tile([P, PARTS, PART], U32, align_bytes=64)
+        w_scales = keep.tile([P, PARTS, PART], U8, align_bytes=64)
+        for q in range(PARTS):
+            for half in range(2):
+                w_turned = psum_g.tile([P, PACK, HALF_TOKENS], BF16, tag="turned_bf")
+                for t in range(PACK):
+                    for a in range(2):
+                        nc.tensor.transpose(
+                            w_turned[:, t, a * P : (a + 1) * P],
+                            w_rows[:, q * PACK + half * 2 + a, t * P : (t + 1) * P],
+                            ident_bf[:],
+                        )
+                nc.vector.tensor_copy(
+                    out=w_grouped[:, q, half * HALF_TOKENS : (half + 1) * HALF_TOKENS, :],
+                    in_=w_turned[:].rearrange("p t i -> p i t"),
+                )
+            nc.vector.quantize_mx(
+                out=w_codes[:, q, :].bitcast(E4M3_X4),
+                scales=w_scales[:, q, :],
+                in_=w_grouped[:, q].rearrange("p i t -> p (i t)"),
+            )
+
+        for c in range(GROUPS):
+            for q in range(PARTS):
+                silu_neg = work.tile([P, PACK, GROUP_TOKENS], F32)
+                c_sig = work.tile([P, PACK, GROUP_TOKENS], F32)
+                for t in range(PACK):
+                    b = q * PACK + t
+                    y_turned = psum_y.tile([P, GROUP_TOKENS], F32)
+                    for j in range(GROUP):
+                        nc.tensor.transpose(
+                            y_turned[:, j * P : (j + 1) * P], y_rows[c, q][:, j, t * P : (t + 1) * P], ident_f32[:]
+                        )
+                    nc.scalar.activation(
+                        out=silu_neg[:, t, :], in_=y_turned[:], func=ACT.Silu, scale=neg_beta_col[:, b : b + 1]
+                    )
+                    nc.scalar.activation(
+                        out=c_sig[:, t, :], in_=y_turned[:], func=ACT.Tanh, scale=half_beta_col[:, b : b + 1]
+                    )
+                    nc.scalar.activation(
+                        out=c_sig[:, t, :],
+                        in_=c_sig[:, t, :],
+                        func=ACT.Identity,
+                        scale=c_col[:, b : b + 1],
+                        bias=c_col[:, b : b + 1],
+                    )
+
+                deriv = work.tile([P, PACK, GROUP_TOKENS], F32)
+                nc.vector.scalar_tensor_tensor(
+                    out=deriv[:].rearrange("p t r -> p (t r)"),
+                    in0=silu_neg[:].rearrange("p t r -> p (t r)"),
+                    scalar=1.0,
+                    in1=c_sig[:].rearrange("p t r -> p (t r)"),
+                    op0=ALU.subtract,
+                    op1=ALU.mult,
+                )
+                for t in range(PACK):
+                    b = q * PACK + t
+                    nc.vector.tensor_scalar(
+                        out=deriv[:, t, :], in0=deriv[:, t, :], scalar1=gamma_col[:, b : b + 1], scalar2=None, op0=ALU.add
+                    )
+
+                dy_grouped = work.tile([P, GROUP_TOKENS, PACK], BF16, align_bytes=64)
+                for half in range(2):
+                    tokens = slice(half * HALF_TOKENS, (half + 1) * HALF_TOKENS)
+                    g_turned = psum_g.tile([P, PACK, HALF_TOKENS], BF16, tag="turned_bf")
+                    for t in range(PACK):
+                        for a in range(2):
+                            nc.tensor.transpose(
+                                g_turned[:, t, a * P : (a + 1) * P],
+                                g_rows[c][:, half * 2 + a, q * PART + t * P : q * PART + (t + 1) * P],
+                                ident_bf[:],
+                            )
+                    nc.vector.tensor_tensor(
+                        out=dy_grouped[:, tokens, :],
+                        in0=deriv[:, :, tokens].rearrange("p t r -> p r t"),
+                        in1=g_turned[:].rearrange("p t r -> p r t"),
+                        op=ALU.mult,
+                    )
+                dy_codes = work.tile([P, GROUP_TOKENS], U32, align_bytes=64)
+                dy_scales = work.tile([P, GROUP_TOKENS], U8, align_bytes=64)
+                nc.vector.quantize_mx(
+                    out=dy_codes[:].bitcast(E5M2_X4),
+                    scales=dy_scales[:],
+                    in_=dy_grouped[:].rearrange("p r t -> p (r t)"),
+                )
+
+                result = work.tile([P, GROUP, PART], F32)
+                for j in range(GROUP):
+                    dx = psum_dx.tile([P, PART], F32)
+                    nc.tensor.matmul_mx(
+                        out=dx[:],
+                        lhsT=dy_codes[:, j * P : (j + 1) * P].bitcast(E5M2_X4),
+                        lhsT_scale=dy_scales[:, j * P : (j + 1) * P],
+                        rhs=w_codes[:, q, :].bitcast(E4M3_X4),
+                        rhs_scale=w_scales[:, q, :],
+                        start=True,
+                        stop=True,
+                    )
+                    nc.vector.scalar_tensor_tensor(
+                        out=result[:, j, :],
+                        in0=dx[:],
+                        scalar=gain_col[:, 0:1],
+                        in1=g_rows[c][:, j, q * PART : (q + 1) * PART],
+                        op0=ALU.mult,
+                        op1=ALU.add,
+                    )
+                nc.sync.dma_start(
+                    out=out_view[:, c * GROUP : (c + 1) * GROUP, q * PART : (q + 1) * PART], in_=result[:]
+                )

@@ -41,9 +41,14 @@ def tile_better_transformer_t_v_kernel(
     with ExitStack() as ctx:
         keep = ctx.enter_context(tc.tile_pool(name="keep", bufs=1))
         work = ctx.enter_context(tc.tile_pool(name="work", bufs=2))
+        store = ctx.enter_context(tc.tile_pool(name="store", bufs=6))
         psum_y = ctx.enter_context(tc.psum_pool(name="psum_y", bufs=4))
         psum_g = ctx.enter_context(tc.psum_pool(name="psum_g", bufs=2))
         psum_dx = ctx.enter_context(tc.psum_pool(name="psum_dx", bufs=2))
+
+        warm = keep.tile([P, 1], F32)
+        nc.vector.memset(warm[:], 0.0)
+        nc.scalar.activation(out=warm[:], in_=warm[:], func=ACT.Silu)
 
         vec_rows = keep.tile([P, P], BF16)
         nc.vector.memset(vec_rows[:], 0.0)
@@ -115,91 +120,135 @@ def tile_better_transformer_t_v_kernel(
                 in_=w_grouped[:, q].rearrange("p i t -> p (i t)"),
             )
 
-        for c in range(GROUPS):
-            for q in range(PARTS):
-                silu_neg = work.tile([P, PACK, GROUP_TOKENS], F32)
-                c_sig = work.tile([P, PACK, GROUP_TOKENS], F32)
-                for t in range(PACK):
-                    b = q * PACK + t
-                    y_turned = psum_y.tile([P, GROUP_TOKENS], F32)
+        units = [(c, q) for c in range(GROUPS) for q in range(PARTS)]
+        silu_neg = {}
+        c_sig = {}
+        product = {}
+        g_turned = {}
+        dy_planes = {}
+        dy_grouped = {}
+        dy_codes = {}
+        dy_scales = {}
+
+        def functions_of_y(u):
+            c, q = units[u]
+            silu_neg[u] = work.tile([P, PACK, GROUP_TOKENS], F32, name="silu_neg_%d" % u, tag="silu_neg")
+            c_sig[u] = work.tile([P, PACK, GROUP_TOKENS], F32, name="c_sig_%d" % u, tag="c_sig")
+            for t in range(PACK):
+                b = q * PACK + t
+                y_turned = psum_y.tile([P, GROUP_TOKENS], F32)
+                for j in range(GROUP):
+                    nc.tensor.transpose(
+                        y_turned[:, j * P : (j + 1) * P], y_rows[c, q][:, j, t * P : (t + 1) * P], ident_f32[:]
+                    )
+                nc.scalar.activation(
+                    out=c_sig[u][:, t, :], in_=y_turned[:], func=ACT.Tanh, scale=half_beta_col[:, b : b + 1]
+                )
+                nc.scalar.activation(
+                    out=silu_neg[u][:, t, :], in_=y_turned[:], func=ACT.Silu, scale=neg_beta_col[:, b : b + 1]
+                )
+                nc.scalar.activation(
+                    out=c_sig[u][:, t, :],
+                    in_=c_sig[u][:, t, :],
+                    func=ACT.Identity,
+                    scale=c_col[:, b : b + 1],
+                    bias=c_col[:, b : b + 1],
+                )
+
+        def turn_grad_out(u):
+            c, q = units[u]
+            for pair in range(2):
+                g_turned[u, pair] = psum_g.tile([P, 2, GROUP_TOKENS], BF16, name="g_turned_%d_%d" % (u, pair), tag="turned_bf")
+                for s in range(2):
+                    first = q * PART + (pair * 2 + s) * P
                     for j in range(GROUP):
                         nc.tensor.transpose(
-                            y_turned[:, j * P : (j + 1) * P], y_rows[c, q][:, j, t * P : (t + 1) * P], ident_f32[:]
+                            g_turned[u, pair][:, s, j * P : (j + 1) * P], g_rows[c][:, j, first : first + P], ident_bf[:]
                         )
-                    nc.scalar.activation(
-                        out=silu_neg[:, t, :], in_=y_turned[:], func=ACT.Silu, scale=neg_beta_col[:, b : b + 1]
-                    )
-                    nc.scalar.activation(
-                        out=c_sig[:, t, :], in_=y_turned[:], func=ACT.Tanh, scale=half_beta_col[:, b : b + 1]
-                    )
-                    nc.scalar.activation(
-                        out=c_sig[:, t, :],
-                        in_=c_sig[:, t, :],
-                        func=ACT.Identity,
-                        scale=c_col[:, b : b + 1],
-                        bias=c_col[:, b : b + 1],
-                    )
 
-                deriv = work.tile([P, PACK, GROUP_TOKENS], F32)
+        def product_of_functions(u):
+            product[u] = work.tile([P, PACK, GROUP_TOKENS], F32, name="product_%d" % u, tag="product")
+            for t in range(PACK):
                 nc.vector.scalar_tensor_tensor(
-                    out=deriv[:].rearrange("p t r -> p (t r)"),
-                    in0=silu_neg[:].rearrange("p t r -> p (t r)"),
+                    out=product[u][:, t, :],
+                    in0=silu_neg[u][:, t, :],
                     scalar=1.0,
-                    in1=c_sig[:].rearrange("p t r -> p (t r)"),
+                    in1=c_sig[u][:, t, :],
                     op0=ALU.subtract,
                     op1=ALU.mult,
                 )
-                for t in range(PACK):
-                    b = q * PACK + t
-                    nc.vector.tensor_scalar(
-                        out=deriv[:, t, :], in0=deriv[:, t, :], scalar1=gamma_col[:, b : b + 1], scalar2=None, op0=ALU.add
-                    )
 
-                dy_grouped = work.tile([P, GROUP_TOKENS, PACK], BF16, align_bytes=64)
-                for half in range(2):
-                    tokens = slice(half * HALF_TOKENS, (half + 1) * HALF_TOKENS)
-                    g_turned = psum_g.tile([P, PACK, HALF_TOKENS], BF16, tag="turned_bf")
-                    for t in range(PACK):
-                        for a in range(2):
-                            nc.tensor.transpose(
-                                g_turned[:, t, a * P : (a + 1) * P],
-                                g_rows[c][:, half * 2 + a, q * PART + t * P : q * PART + (t + 1) * P],
-                                ident_bf[:],
-                            )
-                    nc.vector.tensor_tensor(
-                        out=dy_grouped[:, tokens, :],
-                        in0=deriv[:, :, tokens].rearrange("p t r -> p r t"),
-                        in1=g_turned[:].rearrange("p t r -> p r t"),
-                        op=ALU.mult,
-                    )
-                dy_codes = work.tile([P, GROUP_TOKENS], U32, align_bytes=64)
-                dy_scales = work.tile([P, GROUP_TOKENS], U8, align_bytes=64)
-                nc.vector.quantize_mx(
-                    out=dy_codes[:].bitcast(E5M2_X4),
-                    scales=dy_scales[:],
-                    in_=dy_grouped[:].rearrange("p r t -> p (r t)"),
+        def gradient_of_y(u):
+            q = units[u][1]
+            dy_planes[u] = work.tile([P, PACK, GROUP_TOKENS], BF16, name="dy_planes_%d" % u, tag="dy_planes")
+            for t in range(PACK):
+                b = q * PACK + t
+                nc.vector.scalar_tensor_tensor(
+                    out=dy_planes[u][:, t, :],
+                    in0=product[u][:, t, :],
+                    scalar=gamma_col[:, b : b + 1],
+                    in1=g_turned[u, t // 2][:, t % 2, :],
+                    op0=ALU.add,
+                    op1=ALU.mult,
                 )
 
-                result = work.tile([P, GROUP, PART], F32)
-                for j in range(GROUP):
-                    dx = psum_dx.tile([P, PART], F32)
-                    nc.tensor.matmul_mx(
-                        out=dx[:],
-                        lhsT=dy_codes[:, j * P : (j + 1) * P].bitcast(E5M2_X4),
-                        lhsT_scale=dy_scales[:, j * P : (j + 1) * P],
-                        rhs=w_codes[:, q, :].bitcast(E4M3_X4),
-                        rhs_scale=w_scales[:, q, :],
-                        start=True,
-                        stop=True,
-                    )
-                    nc.vector.scalar_tensor_tensor(
-                        out=result[:, j, :],
-                        in0=dx[:],
-                        scalar=gain_col[:, 0:1],
-                        in1=g_rows[c][:, j, q * PART : (q + 1) * PART],
-                        op0=ALU.mult,
-                        op1=ALU.add,
-                    )
-                nc.sync.dma_start(
-                    out=out_view[:, c * GROUP : (c + 1) * GROUP, q * PART : (q + 1) * PART], in_=result[:]
+        def group_words(u):
+            dy_grouped[u] = work.tile([P, GROUP_TOKENS, PACK], BF16, name="dy_grouped_%d" % u, tag="dy_grouped", align_bytes=64)
+            nc.vector.tensor_copy(
+                out=dy_grouped[u][:, 0:P, :].rearrange("p (n i) t -> p n t i", i=4),
+                in_=dy_planes[u][:, :, 0:P].rearrange("p t (n i) -> p n t i", i=4),
+            )
+            nc.scalar.copy(
+                out=dy_grouped[u][:, P:GROUP_TOKENS, :].rearrange("p (n i) t -> p n t i", i=4),
+                in_=dy_planes[u][:, :, P:GROUP_TOKENS].rearrange("p t (n i) -> p n t i", i=4),
+            )
+
+        def quantise(u):
+            dy_codes[u] = work.tile([P, GROUP_TOKENS], U32, name="dy_codes_%d" % u, tag="dy_codes", align_bytes=64)
+            dy_scales[u] = work.tile([P, GROUP_TOKENS], U8, name="dy_scales_%d" % u, tag="dy_scales", align_bytes=64)
+            nc.vector.quantize_mx(
+                out=dy_codes[u][:].bitcast(E5M2_X4),
+                scales=dy_scales[u][:],
+                in_=dy_grouped[u][:].rearrange("p r t -> p (r t)"),
+            )
+
+        def multiply_and_store(u):
+            c, q = units[u]
+            for j in range(GROUP):
+                dx = psum_dx.tile([P, PART], F32)
+                nc.tensor.matmul_mx(
+                    out=dx[:],
+                    lhsT=dy_codes[u][:, j * P : (j + 1) * P].bitcast(E5M2_X4),
+                    lhsT_scale=dy_scales[u][:, j * P : (j + 1) * P],
+                    rhs=w_codes[:, q, :].bitcast(E4M3_X4),
+                    rhs_scale=w_scales[:, q, :],
+                    start=True,
+                    stop=True,
                 )
+                result = store.tile([P, PART], F32)
+                nc.vector.scalar_tensor_tensor(
+                    out=result[:],
+                    in0=dx[:],
+                    scalar=gain_col[:, 0:1],
+                    in1=g_rows[c][:, j, q * PART : (q + 1) * PART],
+                    op0=ALU.mult,
+                    op1=ALU.add,
+                )
+                nc.sync.dma_start(out=out_view[:, c * GROUP + j, q * PART : (q + 1) * PART], in_=result[:])
+
+        functions_of_y(0)
+        turn_grad_out(0)
+        for u in range(len(units)):
+            if u + 1 < len(units):
+                functions_of_y(u + 1)
+            product_of_functions(u)
+            if u >= 1:
+                quantise(u - 1)
+            gradient_of_y(u)
+            if u >= 1:
+                multiply_and_store(u - 1)
+            group_words(u)
+            if u + 1 < len(units):
+                turn_grad_out(u + 1)
+        quantise(len(units) - 1)
+        multiply_and_store(len(units) - 1)

@@ -21,9 +21,14 @@ FEATURES = PARTS * PART
 BLOCKS = FEATURES // P
 TILES = TOKENS // P
 GROUP = 4
-GROUPS = TILES // GROUP
 GROUP_TOKENS = GROUP * P
-HALF_TOKENS = GROUP_TOKENS // 2
+UNITS = (TILES // GROUP) * PARTS
+PAIR = 2
+PAIR_TOKENS = PAIR * P
+HALVES = UNITS * 2
+W_PIECES = 2 * PARTS
+RUN = 4
+VECTOR_TOKENS = 96
 
 FLOPS = 2 * TOKENS * PART * PART * PARTS
 BYTES = TOKENS * FEATURES * (4 + 2 + 4) + PARTS * PART * PART * 2 + 2 * FEATURES * 2 + 2
@@ -38,13 +43,17 @@ def tile_better_transformer_t_v_kernel(
     g_view = grad_out.rearrange("(p j) f -> p j f", j=TILES)
     out_view = out.rearrange("(p j) f -> p j f", j=TILES)
 
+    def place(u):
+        return (u // PARTS) * GROUP, u % PARTS
+
     with ExitStack() as ctx:
+        ctx.enter_context(tc.manual_schedule())
         keep = ctx.enter_context(tc.tile_pool(name="keep", bufs=1))
-        work = ctx.enter_context(tc.tile_pool(name="work", bufs=2))
+        work = ctx.enter_context(tc.tile_pool(name="work", bufs=3))
         store = ctx.enter_context(tc.tile_pool(name="store", bufs=6))
-        psum_y = ctx.enter_context(tc.psum_pool(name="psum_y", bufs=4))
+        psum_y = ctx.enter_context(tc.psum_pool(name="psum_y", bufs=2 * PAIR))
         psum_g = ctx.enter_context(tc.psum_pool(name="psum_g", bufs=2))
-        psum_dx = ctx.enter_context(tc.psum_pool(name="psum_dx", bufs=2))
+        psum_dx = ctx.enter_context(tc.psum_pool(name="psum_dx", bufs=PAIR))
 
         warm = keep.tile([P, 1], F32)
         nc.vector.memset(warm[:], 0.0)
@@ -60,25 +69,25 @@ def tile_better_transformer_t_v_kernel(
         w_rows = keep.tile([P, PARTS * PACK, PART], BF16)
         y_rows = {}
         g_rows = {}
-        for c in range(GROUPS):
-            tiles = slice(c * GROUP, (c + 1) * GROUP)
-            for q in range(PARTS):
-                y_rows[c, q] = keep.tile([P, GROUP, PART], F32, name="y_rows_%d_%d" % (c, q))
-                nc.sync.dma_start(out=y_rows[c, q][:], in_=y_view[:, tiles, q * PART : (q + 1) * PART])
-                if q == 0:
-                    g_rows[c] = keep.tile([P, GROUP, FEATURES], BF16, name="g_rows_%d" % c)
-                    nc.sync.dma_start(out=g_rows[c][:], in_=g_view[:, tiles, :])
-                    if c == 0:
-                        nc.sync.dma_start(
-                            out=w_rows[:], in_=weights.rearrange("q (a p) o -> p (q a) o", p=P)
-                        )
+        for u in range(UNITS):
+            tile0, q = place(u)
+            tiles = slice(tile0, tile0 + GROUP)
+            for half in range(2):
+                first = q * PART + half * PAIR * P
+                y_rows[2 * u + half] = keep.tile([P, GROUP, PAIR * P], F32, name="y_rows_%d" % (2 * u + half))
+                nc.sync.dma_start(out=y_rows[2 * u + half][:], in_=y_view[:, tiles, first : first + PAIR * P])
+                if half == 0:
+                    g_rows[u] = keep.tile([P, GROUP, PART], BF16, name="g_rows_%d" % u)
+                    nc.sync.dma_start(out=g_rows[u][:], in_=g_view[:, tiles, q * PART : (q + 1) * PART])
+            if u == 0:
+                nc.sync.dma_start(out=w_rows[:], in_=weights.rearrange("q (a p) o -> p (q a) o", p=P))
 
         ident_f32 = keep.tile([P, P], F32)
         make_identity(nc, ident_f32[:])
         ident_bf = keep.tile([P, P], BF16)
         make_identity(nc, ident_bf[:])
 
-        vec_cols = psum_g.tile([P, PACK, HALF_TOKENS], BF16, tag="turned_bf")
+        vec_cols = psum_g.tile([P, PAIR, GROUP_TOKENS], BF16, tag="g_turned")
         nc.tensor.transpose(vec_cols[:, 0, 0:P], vec_rows[:], ident_bf[:])
         gamma_col = keep.tile([P, BLOCKS], F32)
         nc.vector.tensor_copy(out=gamma_col[:], in_=vec_cols[:, 0, 0:BLOCKS])
@@ -100,155 +109,177 @@ def tile_better_transformer_t_v_kernel(
         w_grouped = keep.tile([P, PARTS, PART, PACK], BF16, align_bytes=64)
         w_codes = keep.tile([P, PARTS, PART], U32, align_bytes=64)
         w_scales = keep.tile([P, PARTS, PART], U8, align_bytes=64)
-        for q in range(PARTS):
-            for half in range(2):
-                w_turned = psum_g.tile([P, PACK, HALF_TOKENS], BF16, tag="turned_bf")
-                for t in range(PACK):
-                    for a in range(2):
-                        nc.tensor.transpose(
-                            w_turned[:, t, a * P : (a + 1) * P],
-                            w_rows[:, q * PACK + half * 2 + a, t * P : (t + 1) * P],
-                            ident_bf[:],
-                        )
-                nc.vector.tensor_copy(
-                    out=w_grouped[:, q, half * HALF_TOKENS : (half + 1) * HALF_TOKENS, :],
-                    in_=w_turned[:].rearrange("p t i -> p i t"),
-                )
-            nc.vector.quantize_mx(
-                out=w_codes[:, q, :].bitcast(E4M3_X4),
-                scales=w_scales[:, q, :],
-                in_=w_grouped[:, q].rearrange("p i t -> p (i t)"),
-            )
 
-        units = [(c, q) for c in range(GROUPS) for q in range(PARTS)]
+        def prepare_weights(piece):
+            q, half = piece // 2, piece % 2
+            w_turned = psum_dx.tile([P, PACK, PAIR_TOKENS], BF16, name="w_turned_%d" % piece, tag="dx")
+            for t in range(PACK):
+                for s in range(PAIR):
+                    nc.tensor.transpose(
+                        w_turned[:, t, s * P : (s + 1) * P],
+                        w_rows[:, q * PACK + half * PAIR + s, t * P : (t + 1) * P],
+                        ident_bf[:],
+                    )
+            nc.vector.tensor_copy(
+                out=w_grouped[:, q, half * PAIR_TOKENS : (half + 1) * PAIR_TOKENS, :],
+                in_=w_turned[:].rearrange("p t i -> p i t"),
+            )
+            if half == 1:
+                nc.vector.quantize_mx(
+                    out=w_codes[:, q, :].bitcast(E4M3_X4),
+                    scales=w_scales[:, q, :],
+                    in_=w_grouped[:, q].rearrange("p i t -> p (i t)"),
+                )
+
+        y_turned = {}
+        g_turned = {}
         silu_neg = {}
         c_sig = {}
         product = {}
-        g_turned = {}
         dy_planes = {}
         dy_grouped = {}
         dy_codes = {}
         dy_scales = {}
+        dx = {}
 
-        def functions_of_y(u):
-            c, q = units[u]
-            silu_neg[u] = work.tile([P, PACK, GROUP_TOKENS], F32, name="silu_neg_%d" % u, tag="silu_neg")
-            c_sig[u] = work.tile([P, PACK, GROUP_TOKENS], F32, name="c_sig_%d" % u, tag="c_sig")
-            for t in range(PACK):
-                b = q * PACK + t
-                y_turned = psum_y.tile([P, GROUP_TOKENS], F32)
+        def turn_y(i):
+            for s in range(PAIR):
+                y_turned[i, s] = psum_y.tile([P, GROUP_TOKENS], F32, name="y_turned_%d_%d" % (i, s), tag="y_turned")
                 for j in range(GROUP):
                     nc.tensor.transpose(
-                        y_turned[:, j * P : (j + 1) * P], y_rows[c, q][:, j, t * P : (t + 1) * P], ident_f32[:]
+                        y_turned[i, s][:, j * P : (j + 1) * P], y_rows[i][:, j, s * P : (s + 1) * P], ident_f32[:]
                     )
+
+        def turn_grad_out(i):
+            g_turned[i] = psum_g.tile([P, PAIR, GROUP_TOKENS], BF16, name="g_turned_%d" % i, tag="g_turned")
+            for s in range(PAIR):
+                first = ((i % 2) * PAIR + s) * P
+                for j in range(GROUP):
+                    nc.tensor.transpose(
+                        g_turned[i][:, s, j * P : (j + 1) * P], g_rows[i // 2][:, j, first : first + P], ident_bf[:]
+                    )
+
+        def block_of(i, s):
+            return place(i // 2)[1] * PACK + (i % 2) * PAIR + s
+
+        def functions_of_y(i):
+            silu_neg[i] = work.tile([P, PAIR, GROUP_TOKENS], F32, name="silu_neg_%d" % i, tag="silu_neg")
+            c_sig[i] = work.tile([P, PAIR, GROUP_TOKENS], F32, name="c_sig_%d" % i, tag="c_sig")
+            for s in range(PAIR):
+                b = block_of(i, s)
                 nc.scalar.activation(
-                    out=c_sig[u][:, t, :], in_=y_turned[:], func=ACT.Tanh, scale=half_beta_col[:, b : b + 1]
+                    out=c_sig[i][:, s, :], in_=y_turned[i, s][:], func=ACT.Tanh, scale=half_beta_col[:, b : b + 1]
                 )
                 nc.scalar.activation(
-                    out=silu_neg[u][:, t, :], in_=y_turned[:], func=ACT.Silu, scale=neg_beta_col[:, b : b + 1]
+                    out=silu_neg[i][:, s, :], in_=y_turned[i, s][:], func=ACT.Silu, scale=neg_beta_col[:, b : b + 1]
                 )
                 nc.scalar.activation(
-                    out=c_sig[u][:, t, :],
-                    in_=c_sig[u][:, t, :],
+                    out=c_sig[i][:, s, :],
+                    in_=c_sig[i][:, s, :],
                     func=ACT.Identity,
                     scale=c_col[:, b : b + 1],
                     bias=c_col[:, b : b + 1],
                 )
 
-        def turn_grad_out(u):
-            c, q = units[u]
-            for pair in range(2):
-                g_turned[u, pair] = psum_g.tile([P, 2, GROUP_TOKENS], BF16, name="g_turned_%d_%d" % (u, pair), tag="turned_bf")
-                for s in range(2):
-                    first = q * PART + (pair * 2 + s) * P
-                    for j in range(GROUP):
-                        nc.tensor.transpose(
-                            g_turned[u, pair][:, s, j * P : (j + 1) * P], g_rows[c][:, j, first : first + P], ident_bf[:]
-                        )
+        def product_of_functions(i):
+            product[i] = work.tile([P, PAIR, GROUP_TOKENS], F32, name="product_%d" % i, tag="product")
+            nc.vector.scalar_tensor_tensor(
+                out=product[i][:].rearrange("p s r -> p (s r)"),
+                in0=silu_neg[i][:].rearrange("p s r -> p (s r)"),
+                scalar=1.0,
+                in1=c_sig[i][:].rearrange("p s r -> p (s r)"),
+                op0=ALU.subtract,
+                op1=ALU.mult,
+            )
 
-        def product_of_functions(u):
-            product[u] = work.tile([P, PACK, GROUP_TOKENS], F32, name="product_%d" % u, tag="product")
-            for t in range(PACK):
+        def gradient_of_y(i):
+            u = i // 2
+            if i % 2 == 0:
+                dy_planes[u] = work.tile([P, PACK, GROUP_TOKENS], BF16, name="dy_planes_%d" % u, tag="dy_planes")
+            for s in range(PAIR):
+                b = block_of(i, s)
                 nc.vector.scalar_tensor_tensor(
-                    out=product[u][:, t, :],
-                    in0=silu_neg[u][:, t, :],
-                    scalar=1.0,
-                    in1=c_sig[u][:, t, :],
-                    op0=ALU.subtract,
-                    op1=ALU.mult,
-                )
-
-        def gradient_of_y(u):
-            q = units[u][1]
-            dy_planes[u] = work.tile([P, PACK, GROUP_TOKENS], BF16, name="dy_planes_%d" % u, tag="dy_planes")
-            for t in range(PACK):
-                b = q * PACK + t
-                nc.vector.scalar_tensor_tensor(
-                    out=dy_planes[u][:, t, :],
-                    in0=product[u][:, t, :],
+                    out=dy_planes[u][:, (i % 2) * PAIR + s, :],
+                    in0=product[i][:, s, :],
                     scalar=gamma_col[:, b : b + 1],
-                    in1=g_turned[u, t // 2][:, t % 2, :],
+                    in1=g_turned[i][:, s, :],
                     op0=ALU.add,
                     op1=ALU.mult,
                 )
 
-        def group_words(u):
-            dy_grouped[u] = work.tile([P, GROUP_TOKENS, PACK], BF16, name="dy_grouped_%d" % u, tag="dy_grouped", align_bytes=64)
+        def group_words(i):
+            first = (i % 2) * PAIR_TOKENS
+            dy_grouped[i] = work.tile([P, PAIR_TOKENS, PACK], BF16, name="dy_grouped_%d" % i, tag="dy_grouped", align_bytes=64)
             nc.vector.tensor_copy(
-                out=dy_grouped[u][:, 0:P, :].rearrange("p (n i) t -> p n t i", i=4),
-                in_=dy_planes[u][:, :, 0:P].rearrange("p t (n i) -> p n t i", i=4),
+                out=dy_grouped[i][:, 0:VECTOR_TOKENS, :].rearrange("p (n r) t -> p n t r", r=RUN),
+                in_=dy_planes[i // 2][:, :, first : first + VECTOR_TOKENS].rearrange("p t (n r) -> p n t r", r=RUN),
             )
             nc.scalar.copy(
-                out=dy_grouped[u][:, P:GROUP_TOKENS, :].rearrange("p (n i) t -> p n t i", i=4),
-                in_=dy_planes[u][:, :, P:GROUP_TOKENS].rearrange("p t (n i) -> p n t i", i=4),
+                out=dy_grouped[i][:, VECTOR_TOKENS:PAIR_TOKENS, :].rearrange("p (n r) t -> p n t r", r=RUN),
+                in_=dy_planes[i // 2][:, :, first + VECTOR_TOKENS : first + PAIR_TOKENS].rearrange(
+                    "p t (n r) -> p n t r", r=RUN
+                ),
             )
 
-        def quantise(u):
-            dy_codes[u] = work.tile([P, GROUP_TOKENS], U32, name="dy_codes_%d" % u, tag="dy_codes", align_bytes=64)
-            dy_scales[u] = work.tile([P, GROUP_TOKENS], U8, name="dy_scales_%d" % u, tag="dy_scales", align_bytes=64)
+        def quantise(i):
+            dy_codes[i] = work.tile([P, PAIR_TOKENS], U32, name="dy_codes_%d" % i, tag="dy_codes", align_bytes=64)
+            dy_scales[i] = work.tile([P, PAIR_TOKENS], U8, name="dy_scales_%d" % i, tag="dy_scales", align_bytes=64)
             nc.vector.quantize_mx(
-                out=dy_codes[u][:].bitcast(E5M2_X4),
-                scales=dy_scales[u][:],
-                in_=dy_grouped[u][:].rearrange("p r t -> p (r t)"),
+                out=dy_codes[i][:].bitcast(E5M2_X4),
+                scales=dy_scales[i][:],
+                in_=dy_grouped[i][:].rearrange("p r t -> p (r t)"),
             )
 
-        def multiply_and_store(u):
-            c, q = units[u]
-            for j in range(GROUP):
-                dx = psum_dx.tile([P, PART], F32)
+        def multiply(i):
+            q = place(i // 2)[1]
+            for s in range(PAIR):
+                dx[i, s] = psum_dx.tile([P, PART], F32, name="dx_%d_%d" % (i, s), tag="dx")
                 nc.tensor.matmul_mx(
-                    out=dx[:],
-                    lhsT=dy_codes[u][:, j * P : (j + 1) * P].bitcast(E5M2_X4),
-                    lhsT_scale=dy_scales[u][:, j * P : (j + 1) * P],
+                    out=dx[i, s][:],
+                    lhsT=dy_codes[i][:, s * P : (s + 1) * P].bitcast(E5M2_X4),
+                    lhsT_scale=dy_scales[i][:, s * P : (s + 1) * P],
                     rhs=w_codes[:, q, :].bitcast(E4M3_X4),
                     rhs_scale=w_scales[:, q, :],
                     start=True,
                     stop=True,
                 )
+
+        def add_residual_and_store(i):
+            u = i // 2
+            tile0, q = place(u)
+            for s in range(PAIR):
+                j = (i % 2) * PAIR + s
                 result = store.tile([P, PART], F32)
                 nc.vector.scalar_tensor_tensor(
                     out=result[:],
-                    in0=dx[:],
+                    in0=dx[i, s][:],
                     scalar=gain_col[:, 0:1],
-                    in1=g_rows[c][:, j, q * PART : (q + 1) * PART],
+                    in1=g_rows[u][:, j, :],
                     op0=ALU.mult,
                     op1=ALU.add,
                 )
-                nc.sync.dma_start(out=out_view[:, c * GROUP + j, q * PART : (q + 1) * PART], in_=result[:])
+                nc.sync.dma_start(out=out_view[:, tile0 + j, q * PART : (q + 1) * PART], in_=result[:])
 
-        functions_of_y(0)
-        turn_grad_out(0)
-        for u in range(len(units)):
-            if u + 1 < len(units):
-                functions_of_y(u + 1)
-            product_of_functions(u)
-            if u >= 1:
-                quantise(u - 1)
-            gradient_of_y(u)
-            if u >= 1:
-                multiply_and_store(u - 1)
-            group_words(u)
-            if u + 1 < len(units):
-                turn_grad_out(u + 1)
-        quantise(len(units) - 1)
-        multiply_and_store(len(units) - 1)
+        def live(i):
+            return 0 <= i < HALVES
+
+        turn_y(0)
+        for k in range(HALVES + 4):
+            if live(k - 4):
+                quantise(k - 4)
+                multiply(k - 4)
+            if live(k + 1):
+                turn_y(k + 1)
+            if live(k):
+                turn_grad_out(k)
+                functions_of_y(k)
+            if live(k - 1):
+                product_of_functions(k - 1)
+            if live(k - 3):
+                group_words(k - 3)
+            if live(k - 1):
+                gradient_of_y(k - 1)
+            if live(k - 4):
+                add_residual_and_store(k - 4)
+            if k < W_PIECES:
+                prepare_weights(k)

@@ -27,8 +27,6 @@ PAIR = 2
 PAIR_TOKENS = PAIR * P
 HALVES = UNITS * 2
 W_PIECES = 2 * PARTS
-RUN = 4
-VECTOR_TOKENS = 96
 
 FLOPS = 2 * TOKENS * PART * PART * PARTS
 BYTES = TOKENS * FEATURES * (4 + 2 + 4) + PARTS * PART * PART * 2 + 2 * FEATURES * 2 + 2
@@ -210,15 +208,13 @@ def tile_better_transformer_t_v_kernel(
         def group_words(i):
             first = (i % 2) * PAIR_TOKENS
             dy_grouped[i] = work.tile([P, PAIR_TOKENS, PACK], BF16, name="dy_grouped_%d" % i, tag="dy_grouped", align_bytes=64)
-            nc.vector.tensor_copy(
-                out=dy_grouped[i][:, 0:VECTOR_TOKENS, :].rearrange("p (n r) t -> p n t r", r=RUN),
-                in_=dy_planes[i // 2][:, :, first : first + VECTOR_TOKENS].rearrange("p t (n r) -> p n t r", r=RUN),
-            )
-            nc.scalar.copy(
-                out=dy_grouped[i][:, VECTOR_TOKENS:PAIR_TOKENS, :].rearrange("p (n r) t -> p n t r", r=RUN),
-                in_=dy_planes[i // 2][:, :, first + VECTOR_TOKENS : first + PAIR_TOKENS].rearrange(
-                    "p t (n r) -> p n t r", r=RUN
-                ),
+            nc.gpsimd.tensor_scalar(
+                out=dy_grouped[i][:],
+                in0=dy_planes[i // 2][:, :, first : first + PAIR_TOKENS].rearrange("p t r -> p r t"),
+                scalar1=1.0,
+                scalar2=0.0,
+                op0=ALU.mult,
+                op1=ALU.add,
             )
 
         def quantise(i):

@@ -27,6 +27,8 @@ PAIR = 2
 PAIR_TOKENS = PAIR * P
 HALVES = UNITS * 2
 W_PIECES = 2 * PARTS
+RUN = 4
+VECTOR_TOKENS = 96
 
 FLOPS = 2 * TOKENS * PART * PART * PARTS
 BYTES = TOKENS * FEATURES * (4 + 2 + 4) + PARTS * PART * PART * 2 + 2 * FEATURES * 2 + 2
@@ -208,13 +210,15 @@ def tile_better_transformer_t_v_kernel(
         def group_words(i):
             first = (i % 2) * PAIR_TOKENS
             dy_grouped[i] = work.tile([P, PAIR_TOKENS, PACK], BF16, name="dy_grouped_%d" % i, tag="dy_grouped", align_bytes=64)
-            nc.gpsimd.tensor_scalar(
-                out=dy_grouped[i][:],
-                in0=dy_planes[i // 2][:, :, first : first + PAIR_TOKENS].rearrange("p t r -> p r t"),
-                scalar1=1.0,
-                scalar2=0.0,
-                op0=ALU.mult,
-                op1=ALU.add,
+            nc.vector.tensor_copy(
+                out=dy_grouped[i][:, 0:VECTOR_TOKENS, :].rearrange("p (n r) t -> p n t r", r=RUN),
+                in_=dy_planes[i // 2][:, :, first : first + VECTOR_TOKENS].rearrange("p t (n r) -> p n t r", r=RUN),
+            )
+            nc.scalar.copy(
+                out=dy_grouped[i][:, VECTOR_TOKENS:PAIR_TOKENS, :].rearrange("p (n r) t -> p n t r", r=RUN),
+                in_=dy_planes[i // 2][:, :, first + VECTOR_TOKENS : first + PAIR_TOKENS].rearrange(
+                    "p t (n r) -> p n t r", r=RUN
+                ),
             )
 
         def quantise(i):
@@ -226,10 +230,10 @@ def tile_better_transformer_t_v_kernel(
                 in_=dy_grouped[i][:].rearrange("p r t -> p (r t)"),
             )
 
-        def multiply(i):
+        def multiply(i, banks, tag):
             q = place(i // 2)[1]
             for s in range(PAIR):
-                dx[i, s] = psum_dx.tile([P, PART], F32, name="dx_%d_%d" % (i, s), tag="dx")
+                dx[i, s] = banks.tile([P, PART], F32, name="dx_%d_%d" % (i, s), tag=tag)
                 nc.tensor.matmul_mx(
                     out=dx[i, s][:],
                     lhsT=dy_codes[i][:, s * P : (s + 1) * P].bitcast(E5M2_X4),
@@ -260,15 +264,14 @@ def tile_better_transformer_t_v_kernel(
             return 0 <= i < HALVES
 
         turn_y(0)
-        for k in range(HALVES + 4):
+        for k in range(HALVES):
             if live(k - 4):
                 quantise(k - 4)
-                multiply(k - 4)
+                multiply(k - 4, psum_dx, "dx")
             if live(k + 1):
                 turn_y(k + 1)
-            if live(k):
-                turn_grad_out(k)
-                functions_of_y(k)
+            turn_grad_out(k)
+            functions_of_y(k)
             if live(k - 1):
                 product_of_functions(k - 1)
             if live(k - 3):
@@ -279,3 +282,22 @@ def tile_better_transformer_t_v_kernel(
                 add_residual_and_store(k - 4)
             if k < W_PIECES:
                 prepare_weights(k)
+
+        last = HALVES - 1
+        quantise(last - 3)
+        multiply(last - 3, psum_dx, "dx")
+        product_of_functions(last)
+        group_words(last - 2)
+        gradient_of_y(last)
+        group_words(last - 1)
+        group_words(last)
+        quantise(last - 2)
+        multiply(last - 2, psum_y, "y_turned")
+        add_residual_and_store(last - 3)
+        quantise(last - 1)
+        multiply(last - 1, psum_y, "y_turned")
+        add_residual_and_store(last - 2)
+        quantise(last)
+        multiply(last, psum_dx, "dx")
+        add_residual_and_store(last - 1)
+        add_residual_and_store(last)

@@ -28,7 +28,6 @@ PAIR_TOKENS = PAIR * P
 HALVES = UNITS * 2
 W_PIECES = 2 * PARTS
 RUN = 4
-VECTOR_TOKENS = 96
 
 FLOPS = 2 * TOKENS * PART * PART * PARTS
 BYTES = TOKENS * FEATURES * (4 + 2 + 4) + PARTS * PART * PART * 2 + 2 * FEATURES * 2 + 2
@@ -51,6 +50,7 @@ def tile_better_transformer_t_v_kernel(
         keep = ctx.enter_context(tc.tile_pool(name="keep", bufs=1))
         work = ctx.enter_context(tc.tile_pool(name="work", bufs=3))
         store = ctx.enter_context(tc.tile_pool(name="store", bufs=6))
+        turn = ctx.enter_context(tc.tile_pool(name="turn", bufs=1))
         psum_y = ctx.enter_context(tc.psum_pool(name="psum_y", bufs=2 * PAIR))
         psum_g = ctx.enter_context(tc.psum_pool(name="psum_g", bufs=2))
         psum_dx = ctx.enter_context(tc.psum_pool(name="psum_dx", bufs=PAIR))
@@ -89,19 +89,15 @@ def tile_better_transformer_t_v_kernel(
 
         vec_cols = psum_g.tile([P, PAIR, GROUP_TOKENS], BF16, tag="g_turned")
         nc.tensor.transpose(vec_cols[:, 0, 0:P], vec_rows[:], ident_bf[:])
-        gamma_col = keep.tile([P, BLOCKS], F32)
-        nc.vector.tensor_copy(out=gamma_col[:], in_=vec_cols[:, 0, 0:BLOCKS])
         c_col = keep.tile([P, BLOCKS], F32)
         nc.vector.tensor_scalar(
-            out=c_col[:], in0=vec_cols[:, 0, 0:BLOCKS], scalar1=1.0, scalar2=0.5, op0=ALU.subtract, op1=ALU.mult
+            out=c_col[:], in0=vec_cols[:, 0, 0:BLOCKS], scalar1=-0.5, scalar2=0.5, op0=ALU.mult, op1=ALU.add
         )
-        neg_beta_col = keep.tile([P, BLOCKS], F32)
+        beta_col = keep.tile([P, BLOCKS], F32)
+        nc.vector.tensor_copy(out=beta_col[:], in_=vec_cols[:, 0, BLOCKS : 2 * BLOCKS])
+        neg_half_beta_col = keep.tile([P, BLOCKS], F32)
         nc.vector.tensor_scalar(
-            out=neg_beta_col[:], in0=vec_cols[:, 0, BLOCKS : 2 * BLOCKS], scalar1=-1.0, scalar2=None, op0=ALU.mult
-        )
-        half_beta_col = keep.tile([P, BLOCKS], F32)
-        nc.vector.tensor_scalar(
-            out=half_beta_col[:], in0=vec_cols[:, 0, BLOCKS : 2 * BLOCKS], scalar1=0.5, scalar2=None, op0=ALU.mult
+            out=neg_half_beta_col[:], in0=vec_cols[:, 0, BLOCKS : 2 * BLOCKS], scalar1=-0.5, scalar2=None, op0=ALU.mult
         )
         gain_col = keep.tile([P, 1], F32)
         nc.vector.tensor_copy(out=gain_col[:], in_=gain_bf[:])
@@ -133,7 +129,8 @@ def tile_better_transformer_t_v_kernel(
 
         y_turned = {}
         g_turned = {}
-        silu_neg = {}
+        silu = {}
+        tanh = {}
         c_sig = {}
         product = {}
         dy_planes = {}
@@ -162,30 +159,40 @@ def tile_better_transformer_t_v_kernel(
         def block_of(i, s):
             return place(i // 2)[1] * PACK + (i % 2) * PAIR + s
 
-        def functions_of_y(i):
-            silu_neg[i] = work.tile([P, PAIR, GROUP_TOKENS], F32, name="silu_neg_%d" % i, tag="silu_neg")
-            c_sig[i] = work.tile([P, PAIR, GROUP_TOKENS], F32, name="c_sig_%d" % i, tag="c_sig")
+        def tanh_of_y(i):
+            tanh[i] = work.tile([P, PAIR, GROUP_TOKENS], F32, name="tanh_%d" % i, tag="tanh")
             for s in range(PAIR):
                 b = block_of(i, s)
                 nc.scalar.activation(
-                    out=c_sig[i][:, s, :], in_=y_turned[i, s][:], func=ACT.Tanh, scale=half_beta_col[:, b : b + 1]
+                    out=tanh[i][:, s, :], in_=y_turned[i, s][:], func=ACT.Tanh, scale=neg_half_beta_col[:, b : b + 1]
                 )
+
+        def silu_of_y(i):
+            silu[i] = work.tile([P, PAIR, GROUP_TOKENS], F32, name="silu_%d" % i, tag="silu")
+            for s in range(PAIR):
+                b = block_of(i, s)
                 nc.scalar.activation(
-                    out=silu_neg[i][:, s, :], in_=y_turned[i, s][:], func=ACT.Silu, scale=neg_beta_col[:, b : b + 1]
+                    out=silu[i][:, s, :], in_=y_turned[i, s][:], func=ACT.Silu, scale=beta_col[:, b : b + 1]
                 )
-                nc.scalar.activation(
+
+        def scale_tanh(i):
+            c_sig[i] = turn.tile([P, PAIR, GROUP_TOKENS], F32, name="c_sig_%d" % i, tag="c_sig")
+            for s in range(PAIR):
+                b = block_of(i, s)
+                nc.gpsimd.tensor_scalar(
                     out=c_sig[i][:, s, :],
-                    in_=c_sig[i][:, s, :],
-                    func=ACT.Identity,
-                    scale=c_col[:, b : b + 1],
-                    bias=c_col[:, b : b + 1],
+                    in0=tanh[i][:, s, :],
+                    scalar1=c_col[:, b : b + 1],
+                    scalar2=c_col[:, b : b + 1],
+                    op0=ALU.mult,
+                    op1=ALU.add,
                 )
 
         def product_of_functions(i):
             product[i] = work.tile([P, PAIR, GROUP_TOKENS], F32, name="product_%d" % i, tag="product")
             nc.vector.scalar_tensor_tensor(
                 out=product[i][:].rearrange("p s r -> p (s r)"),
-                in0=silu_neg[i][:].rearrange("p s r -> p (s r)"),
+                in0=silu[i][:].rearrange("p s r -> p (s r)"),
                 scalar=1.0,
                 in1=c_sig[i][:].rearrange("p s r -> p (s r)"),
                 op0=ALU.subtract,
@@ -196,29 +203,23 @@ def tile_better_transformer_t_v_kernel(
             u = i // 2
             if i % 2 == 0:
                 dy_planes[u] = work.tile([P, PACK, GROUP_TOKENS], BF16, name="dy_planes_%d" % u, tag="dy_planes")
-            for s in range(PAIR):
-                b = block_of(i, s)
-                nc.vector.scalar_tensor_tensor(
-                    out=dy_planes[u][:, (i % 2) * PAIR + s, :],
-                    in0=product[i][:, s, :],
-                    scalar=gamma_col[:, b : b + 1],
-                    in1=g_turned[i][:, s, :],
-                    op0=ALU.add,
-                    op1=ALU.mult,
-                )
-
-        def group_words(i):
-            first = (i % 2) * PAIR_TOKENS
-            dy_grouped[i] = work.tile([P, PAIR_TOKENS, PACK], BF16, name="dy_grouped_%d" % i, tag="dy_grouped", align_bytes=64)
-            nc.vector.tensor_copy(
-                out=dy_grouped[i][:, 0:VECTOR_TOKENS, :].rearrange("p (n r) t -> p n t r", r=RUN),
-                in_=dy_planes[i // 2][:, :, first : first + VECTOR_TOKENS].rearrange("p t (n r) -> p n t r", r=RUN),
+            nc.vector.scalar_tensor_tensor(
+                out=dy_planes[u][:, (i % 2) * PAIR : (i % 2 + 1) * PAIR, :].rearrange("p s r -> p (s r)"),
+                in0=product[i][:].rearrange("p s r -> p (s r)"),
+                scalar=1.0,
+                in1=g_turned[i][:].rearrange("p s r -> p (s r)"),
+                op0=ALU.add,
+                op1=ALU.mult,
             )
-            nc.scalar.copy(
-                out=dy_grouped[i][:, VECTOR_TOKENS:PAIR_TOKENS, :].rearrange("p (n r) t -> p n t r", r=RUN),
-                in_=dy_planes[i // 2][:, :, first + VECTOR_TOKENS : first + PAIR_TOKENS].rearrange(
-                    "p t (n r) -> p n t r", r=RUN
-                ),
+
+        def new_words(i):
+            dy_grouped[i] = work.tile([P, PAIR_TOKENS, PACK], BF16, name="dy_grouped_%d" % i, tag="dy_grouped", align_bytes=64)
+
+        def group_words(engine_copy, i, start, stop):
+            first = (i % 2) * PAIR_TOKENS
+            engine_copy(
+                out=dy_grouped[i][:, start:stop, :].rearrange("p (n r) t -> p n t r", r=RUN),
+                in_=dy_planes[i // 2][:, :, first + start : first + stop].rearrange("p t (n r) -> p n t r", r=RUN),
             )
 
         def quantise(i):
@@ -230,10 +231,10 @@ def tile_better_transformer_t_v_kernel(
                 in_=dy_grouped[i][:].rearrange("p r t -> p (r t)"),
             )
 
-        def multiply(i, banks, tag):
+        def multiply(i):
             q = place(i // 2)[1]
             for s in range(PAIR):
-                dx[i, s] = banks.tile([P, PART], F32, name="dx_%d_%d" % (i, s), tag=tag)
+                dx[i, s] = psum_dx.tile([P, PART], F32, name="dx_%d_%d" % (i, s), tag="dx")
                 nc.tensor.matmul_mx(
                     out=dx[i, s][:],
                     lhsT=dy_codes[i][:, s * P : (s + 1) * P].bitcast(E5M2_X4),
@@ -244,60 +245,49 @@ def tile_better_transformer_t_v_kernel(
                     stop=True,
                 )
 
-        def add_residual_and_store(i):
+        def add_residual_and_store(i, s):
             u = i // 2
             tile0, q = place(u)
-            for s in range(PAIR):
-                j = (i % 2) * PAIR + s
-                result = store.tile([P, PART], F32)
-                nc.vector.scalar_tensor_tensor(
-                    out=result[:],
-                    in0=dx[i, s][:],
-                    scalar=gain_col[:, 0:1],
-                    in1=g_rows[u][:, j, :],
-                    op0=ALU.mult,
-                    op1=ALU.add,
-                )
-                nc.sync.dma_start(out=out_view[:, tile0 + j, q * PART : (q + 1) * PART], in_=result[:])
+            j = (i % 2) * PAIR + s
+            result = store.tile([P, PART], F32, name="result_%d_%d" % (i, s), tag="result")
+            nc.vector.scalar_tensor_tensor(
+                out=result[:],
+                in0=dx[i, s][:],
+                scalar=gain_col[:, 0:1],
+                in1=g_rows[u][:, j, :],
+                op0=ALU.mult,
+                op1=ALU.add,
+            )
+            nc.sync.dma_start(out=out_view[:, tile0 + j, q * PART : (q + 1) * PART], in_=result[:])
 
         def live(i):
             return 0 <= i < HALVES
 
         turn_y(0)
-        for k in range(HALVES):
-            if live(k - 4):
-                quantise(k - 4)
-                multiply(k - 4, psum_dx, "dx")
+        for k in range(HALVES + 5):
             if live(k + 1):
                 turn_y(k + 1)
-            turn_grad_out(k)
-            functions_of_y(k)
+            if live(k):
+                turn_grad_out(k)
+                tanh_of_y(k)
+            if live(k - 3):
+                new_words(k - 3)
+                group_words(nc.scalar.copy, k - 3, 0, PAIR_TOKENS)
+            if live(k):
+                silu_of_y(k)
+            if live(k - 4):
+                quantise(k - 4)
+                multiply(k - 4)
             if live(k - 1):
                 product_of_functions(k - 1)
-            if live(k - 3):
-                group_words(k - 3)
+            if live(k):
+                scale_tanh(k)
+            if live(k - 4):
+                add_residual_and_store(k - 4, 0)
             if live(k - 1):
                 gradient_of_y(k - 1)
+            if k in (1, 2):
+                prepare_weights(2 * (k - 1))
+                prepare_weights(2 * (k - 1) + 1)
             if live(k - 4):
-                add_residual_and_store(k - 4)
-            if k < W_PIECES:
-                prepare_weights(k)
-
-        last = HALVES - 1
-        quantise(last - 3)
-        multiply(last - 3, psum_dx, "dx")
-        product_of_functions(last)
-        group_words(last - 2)
-        gradient_of_y(last)
-        group_words(last - 1)
-        group_words(last)
-        quantise(last - 2)
-        multiply(last - 2, psum_y, "y_turned")
-        add_residual_and_store(last - 3)
-        quantise(last - 1)
-        multiply(last - 1, psum_y, "y_turned")
-        add_residual_and_store(last - 2)
-        quantise(last)
-        multiply(last, psum_dx, "dx")
-        add_residual_and_store(last - 1)
-        add_residual_and_store(last)
+                add_residual_and_store(k - 4, 1)

@@ -27,7 +27,7 @@ PAIR = 2
 PAIR_TOKENS = PAIR * P
 HALVES = UNITS * 2
 W_PIECES = 2 * PARTS
-RUN = 4
+EARLY = 3
 
 FLOPS = 2 * TOKENS * PART * PART * PARTS
 BYTES = TOKENS * FEATURES * (4 + 2 + 4) + PARTS * PART * PART * 2 + 2 * FEATURES * 2 + 2
@@ -50,7 +50,6 @@ def tile_better_transformer_t_v_kernel(
         keep = ctx.enter_context(tc.tile_pool(name="keep", bufs=1))
         work = ctx.enter_context(tc.tile_pool(name="work", bufs=3))
         store = ctx.enter_context(tc.tile_pool(name="store", bufs=6))
-        turn = ctx.enter_context(tc.tile_pool(name="turn", bufs=1))
         psum_y = ctx.enter_context(tc.psum_pool(name="psum_y", bufs=2 * PAIR))
         psum_g = ctx.enter_context(tc.psum_pool(name="psum_g", bufs=2))
         psum_dx = ctx.enter_context(tc.psum_pool(name="psum_dx", bufs=PAIR))
@@ -130,10 +129,9 @@ def tile_better_transformer_t_v_kernel(
         y_turned = {}
         g_turned = {}
         silu = {}
-        tanh = {}
         c_sig = {}
         product = {}
-        dy_planes = {}
+        dy_pairs = {}
         dy_grouped = {}
         dy_codes = {}
         dy_scales = {}
@@ -159,29 +157,32 @@ def tile_better_transformer_t_v_kernel(
         def block_of(i, s):
             return place(i // 2)[1] * PACK + (i % 2) * PAIR + s
 
-        def tanh_of_y(i):
-            tanh[i] = work.tile([P, PAIR, GROUP_TOKENS], F32, name="tanh_%d" % i, tag="tanh")
+        def functions_of_y(i):
+            silu[i] = work.tile([P, PAIR, GROUP_TOKENS], F32, name="silu_%d" % i, tag="silu")
+            c_sig[i] = work.tile([P, PAIR, GROUP_TOKENS], F32, name="c_sig_%d" % i, tag="c_sig")
             for s in range(PAIR):
                 b = block_of(i, s)
                 nc.scalar.activation(
-                    out=tanh[i][:, s, :], in_=y_turned[i, s][:], func=ACT.Tanh, scale=neg_half_beta_col[:, b : b + 1]
+                    out=c_sig[i][:, s, :], in_=y_turned[i, s][:], func=ACT.Tanh, scale=neg_half_beta_col[:, b : b + 1]
                 )
-
-        def silu_of_y(i):
-            silu[i] = work.tile([P, PAIR, GROUP_TOKENS], F32, name="silu_%d" % i, tag="silu")
-            for s in range(PAIR):
-                b = block_of(i, s)
                 nc.scalar.activation(
                     out=silu[i][:, s, :], in_=y_turned[i, s][:], func=ACT.Silu, scale=beta_col[:, b : b + 1]
                 )
+                if i >= EARLY:
+                    nc.scalar.activation(
+                        out=c_sig[i][:, s, :],
+                        in_=c_sig[i][:, s, :],
+                        func=ACT.Identity,
+                        scale=c_col[:, b : b + 1],
+                        bias=c_col[:, b : b + 1],
+                    )
 
-        def scale_tanh(i):
-            c_sig[i] = turn.tile([P, PAIR, GROUP_TOKENS], F32, name="c_sig_%d" % i, tag="c_sig")
+        def scale_tanh_on_vector(i):
             for s in range(PAIR):
                 b = block_of(i, s)
-                nc.gpsimd.tensor_scalar(
+                nc.vector.tensor_scalar(
                     out=c_sig[i][:, s, :],
-                    in0=tanh[i][:, s, :],
+                    in0=c_sig[i][:, s, :],
                     scalar1=c_col[:, b : b + 1],
                     scalar2=c_col[:, b : b + 1],
                     op0=ALU.mult,
@@ -202,24 +203,25 @@ def tile_better_transformer_t_v_kernel(
         def gradient_of_y(i):
             u = i // 2
             if i % 2 == 0:
-                dy_planes[u] = work.tile([P, PACK, GROUP_TOKENS], BF16, name="dy_planes_%d" % u, tag="dy_planes")
+                dy_pairs[u] = work.tile([P, PAIR, GROUP_TOKENS, PAIR], BF16, name="dy_pairs_%d" % u, tag="dy_pairs")
             nc.vector.scalar_tensor_tensor(
-                out=dy_planes[u][:, (i % 2) * PAIR : (i % 2 + 1) * PAIR, :].rearrange("p s r -> p (s r)"),
-                in0=product[i][:].rearrange("p s r -> p (s r)"),
+                out=dy_pairs[u][:, i % 2, :, :],
+                in0=product[i][:].rearrange("p s r -> p r s"),
                 scalar=1.0,
-                in1=g_turned[i][:].rearrange("p s r -> p (s r)"),
+                in1=g_turned[i][:].rearrange("p s r -> p r s"),
                 op0=ALU.add,
                 op1=ALU.mult,
             )
 
-        def new_words(i):
-            dy_grouped[i] = work.tile([P, PAIR_TOKENS, PACK], BF16, name="dy_grouped_%d" % i, tag="dy_grouped", align_bytes=64)
-
-        def group_words(engine_copy, i, start, stop):
+        def merge_pairs(i):
             first = (i % 2) * PAIR_TOKENS
-            engine_copy(
-                out=dy_grouped[i][:, start:stop, :].rearrange("p (n r) t -> p n t r", r=RUN),
-                in_=dy_planes[i // 2][:, :, first + start : first + stop].rearrange("p t (n r) -> p n t r", r=RUN),
+            dy_grouped[i] = work.tile([P, PAIR_TOKENS, PACK], BF16, name="dy_grouped_%d" % i, tag="dy_grouped", align_bytes=64)
+            nc.scalar.copy(
+                out=dy_grouped[i][:].rearrange("p r t -> p (r t)").bitcast(F32).rearrange("p (r h) -> p r h", h=PAIR),
+                in_=dy_pairs[i // 2][:]
+                .rearrange("p h r s -> p h (r s)")
+                .bitcast(F32)[:, :, first : first + PAIR_TOKENS]
+                .rearrange("p h r -> p r h"),
             )
 
         def quantise(i):
@@ -231,10 +233,10 @@ def tile_better_transformer_t_v_kernel(
                 in_=dy_grouped[i][:].rearrange("p r t -> p (r t)"),
             )
 
-        def multiply(i):
+        def multiply(i, banks, tag):
             q = place(i // 2)[1]
             for s in range(PAIR):
-                dx[i, s] = psum_dx.tile([P, PART], F32, name="dx_%d_%d" % (i, s), tag="dx")
+                dx[i, s] = banks.tile([P, PART], F32, name="dx_%d_%d" % (i, s), tag=tag)
                 nc.tensor.matmul_mx(
                     out=dx[i, s][:],
                     lhsT=dy_codes[i][:, s * P : (s + 1) * P].bitcast(E5M2_X4),
@@ -264,24 +266,20 @@ def tile_better_transformer_t_v_kernel(
             return 0 <= i < HALVES
 
         turn_y(0)
-        for k in range(HALVES + 5):
+        for k in range(HALVES):
             if live(k + 1):
                 turn_y(k + 1)
-            if live(k):
-                turn_grad_out(k)
-                tanh_of_y(k)
+            turn_grad_out(k)
+            functions_of_y(k)
             if live(k - 3):
-                new_words(k - 3)
-                group_words(nc.scalar.copy, k - 3, 0, PAIR_TOKENS)
-            if live(k):
-                silu_of_y(k)
+                merge_pairs(k - 3)
             if live(k - 4):
                 quantise(k - 4)
-                multiply(k - 4)
+                multiply(k - 4, psum_dx, "dx")
             if live(k - 1):
                 product_of_functions(k - 1)
-            if live(k):
-                scale_tanh(k)
+            if k < EARLY:
+                scale_tanh_on_vector(k)
             if live(k - 4):
                 add_residual_and_store(k - 4, 0)
             if live(k - 1):
@@ -291,3 +289,26 @@ def tile_better_transformer_t_v_kernel(
                 prepare_weights(2 * (k - 1) + 1)
             if live(k - 4):
                 add_residual_and_store(k - 4, 1)
+
+        last = HALVES - 1
+        merge_pairs(last - 2)
+        product_of_functions(last)
+        quantise(last - 3)
+        multiply(last - 3, psum_dx, "dx")
+        gradient_of_y(last)
+        merge_pairs(last - 1)
+        merge_pairs(last)
+        quantise(last - 2)
+        multiply(last - 2, psum_y, "y_turned")
+        add_residual_and_store(last - 3, 0)
+        add_residual_and_store(last - 3, 1)
+        quantise(last - 1)
+        multiply(last - 1, psum_y, "y_turned")
+        add_residual_and_store(last - 2, 0)
+        add_residual_and_store(last - 2, 1)
+        quantise(last)
+        multiply(last, psum_dx, "dx")
+        add_residual_and_store(last - 1, 0)
+        add_residual_and_store(last - 1, 1)
+        add_residual_and_store(last, 0)
+        add_residual_and_store(last, 1)

@@ -49,7 +49,7 @@ def tile_better_transformer_t_v_kernel(
         ctx.enter_context(tc.manual_schedule())
         keep = ctx.enter_context(tc.tile_pool(name="keep", bufs=1))
         work = ctx.enter_context(tc.tile_pool(name="work", bufs=3))
-        store = ctx.enter_context(tc.tile_pool(name="store", bufs=6))
+        store = ctx.enter_context(tc.tile_pool(name="store", bufs=2 * GROUP))
         psum_y = ctx.enter_context(tc.psum_pool(name="psum_y", bufs=2 * PAIR))
         psum_g = ctx.enter_context(tc.psum_pool(name="psum_g", bufs=2))
         psum_dx = ctx.enter_context(tc.psum_pool(name="psum_dx", bufs=PAIR))
@@ -71,15 +71,28 @@ def tile_better_transformer_t_v_kernel(
         for u in range(UNITS):
             tile0, q = place(u)
             tiles = slice(tile0, tile0 + GROUP)
-            for half in range(2):
-                first = q * PART + half * PAIR * P
-                y_rows[2 * u + half] = keep.tile([P, GROUP, PAIR * P], F32, name="y_rows_%d" % (2 * u + half))
-                nc.sync.dma_start(out=y_rows[2 * u + half][:], in_=y_view[:, tiles, first : first + PAIR * P])
-                if half == 0:
-                    g_rows[u] = keep.tile([P, GROUP, PART], BF16, name="g_rows_%d" % u)
-                    nc.sync.dma_start(out=g_rows[u][:], in_=g_view[:, tiles, q * PART : (q + 1) * PART])
-            if u == 0:
-                nc.sync.dma_start(out=w_rows[:], in_=weights.rearrange("q (a p) o -> p (q a) o", p=P))
+            if u < PARTS:
+                for half in range(2):
+                    first = q * PART + half * PAIR * P
+                    y_piece = keep.tile([P, GROUP, PAIR * P], F32, name="y_rows_%d_%d" % (u, half))
+                    nc.sync.dma_start(out=y_piece[:], in_=y_view[:, tiles, first : first + PAIR * P])
+                    y_rows[2 * u + half] = y_piece[:]
+                    if half == 0:
+                        g_piece = keep.tile([P, GROUP, PART], BF16, name="g_rows_%d" % u)
+                        nc.sync.dma_start(out=g_piece[:], in_=g_view[:, tiles, q * PART : (q + 1) * PART])
+                        g_rows[u] = g_piece[:]
+                if u == 0:
+                    nc.sync.dma_start(out=w_rows[:], in_=weights.rearrange("q (a p) o -> p (q a) o", p=P))
+            else:
+                y_unit = keep.tile([P, GROUP, PART], F32, name="y_rows_%d" % u)
+                nc.sync.dma_start(out=y_unit[:], in_=y_view[:, tiles, q * PART : (q + 1) * PART])
+                for half in range(2):
+                    y_rows[2 * u + half] = y_unit[:, :, half * PAIR * P : (half + 1) * PAIR * P]
+                if q == 0:
+                    g_group = keep.tile([P, GROUP, FEATURES], BF16, name="g_rows_%d" % u)
+                    nc.sync.dma_start(out=g_group[:], in_=g_view[:, tiles, :])
+                    for part in range(PARTS):
+                        g_rows[u + part] = g_group[:, :, part * PART : (part + 1) * PART]
 
         ident_f32 = keep.tile([P, P], F32)
         make_identity(nc, ident_f32[:])
@@ -136,6 +149,7 @@ def tile_better_transformer_t_v_kernel(
         dy_codes = {}
         dy_scales = {}
         dx = {}
+        result = {}
 
         def turn_y(i):
             for s in range(PAIR):
@@ -251,16 +265,22 @@ def tile_better_transformer_t_v_kernel(
             u = i // 2
             tile0, q = place(u)
             j = (i % 2) * PAIR + s
-            result = store.tile([P, PART], F32, name="result_%d_%d" % (i, s), tag="result")
+            if q == 0:
+                result[tile0 + j] = store.tile([P, FEATURES], F32, name="result_%d" % (tile0 + j), tag="result")
             nc.vector.scalar_tensor_tensor(
-                out=result[:],
+                out=result[tile0 + j][:, q * PART : (q + 1) * PART],
                 in0=dx[i, s][:],
                 scalar=gain_col[:, 0:1],
                 in1=g_rows[u][:, j, :],
                 op0=ALU.mult,
                 op1=ALU.add,
             )
-            nc.sync.dma_start(out=out_view[:, tile0 + j, q * PART : (q + 1) * PART], in_=result[:])
+            if u >= UNITS - PARTS:
+                nc.sync.dma_start(
+                    out=out_view[:, tile0 + j, q * PART : (q + 1) * PART], in_=result[tile0 + j][:, q * PART : (q + 1) * PART]
+                )
+            elif q == PARTS - 1:
+                nc.sync.dma_start(out=out_view[:, tile0 + j, :], in_=result[tile0 + j][:])
 
         def live(i):
             return 0 <= i < HALVES

@@ -65,7 +65,7 @@ def tile_better_transformer_t_v_kernel(
         gain_bf = keep.tile([P, 1], BF16)
         nc.scalar.dma_start(out=gain_bf[:], in_=gain.partition_broadcast(P))
 
-        w_rows = keep.tile([P, PARTS * PACK, PART], BF16)
+        w_rows = {}
         y_rows = {}
         g_rows = {}
         for u in range(UNITS):
@@ -77,12 +77,12 @@ def tile_better_transformer_t_v_kernel(
                     y_piece = keep.tile([P, GROUP, PAIR * P], F32, name="y_rows_%d_%d" % (u, half))
                     nc.sync.dma_start(out=y_piece[:], in_=y_view[:, tiles, first : first + PAIR * P])
                     y_rows[2 * u + half] = y_piece[:]
-                    if half == 0:
+                    if half == u:
                         g_piece = keep.tile([P, GROUP, PART], BF16, name="g_rows_%d" % u)
                         nc.sync.dma_start(out=g_piece[:], in_=g_view[:, tiles, q * PART : (q + 1) * PART])
                         g_rows[u] = g_piece[:]
-                if u == 0:
-                    nc.sync.dma_start(out=w_rows[:], in_=weights.rearrange("q (a p) o -> p (q a) o", p=P))
+                w_rows[q] = keep.tile([P, PACK, PART], BF16, name="w_rows_%d" % q)
+                nc.sync.dma_start(out=w_rows[q][:], in_=weights[q].rearrange("(a p) o -> p a o", p=P))
             else:
                 y_unit = keep.tile([P, GROUP, PART], F32, name="y_rows_%d" % u)
                 nc.sync.dma_start(out=y_unit[:], in_=y_view[:, tiles, q * PART : (q + 1) * PART])
@@ -112,7 +112,6 @@ def tile_better_transformer_t_v_kernel(
             out=neg_half_beta_col[:], in0=vec_cols[:, 0, BLOCKS : 2 * BLOCKS], scalar1=-0.5, scalar2=None, op0=ALU.mult
         )
         gain_col = keep.tile([P, 1], F32)
-        nc.vector.tensor_copy(out=gain_col[:], in_=gain_bf[:])
 
         w_grouped = keep.tile([P, PARTS, PART, PACK], BF16, align_bytes=64)
         w_codes = keep.tile([P, PARTS, PART], U32, align_bytes=64)
@@ -125,7 +124,7 @@ def tile_better_transformer_t_v_kernel(
                 for s in range(PAIR):
                     nc.tensor.transpose(
                         w_turned[:, t, s * P : (s + 1) * P],
-                        w_rows[:, q * PACK + half * PAIR + s, t * P : (t + 1) * P],
+                        w_rows[q][:, half * PAIR + s, t * P : (t + 1) * P],
                         ident_bf[:],
                     )
             nc.vector.tensor_copy(
@@ -304,9 +303,11 @@ def tile_better_transformer_t_v_kernel(
                 add_residual_and_store(k - 4, 0)
             if live(k - 1):
                 gradient_of_y(k - 1)
-            if k in (1, 2):
-                prepare_weights(2 * (k - 1))
-                prepare_weights(2 * (k - 1) + 1)
+            if k in (2, 3):
+                prepare_weights(2 * (k - 2))
+                prepare_weights(2 * (k - 2) + 1)
+            if k == 3:
+                nc.vector.tensor_copy(out=gain_col[:], in_=gain_bf[:])
             if live(k - 4):
                 add_residual_and_store(k - 4, 1)
 

@@ -27,6 +27,7 @@ PAIR = 2
 PAIR_TOKENS = PAIR * P
 HALVES = UNITS * 2
 W_PIECES = 2 * PARTS
+GAIN_ROW = 32
 EARLY = 3
 
 FLOPS = 2 * TOKENS * PART * PART * PARTS
@@ -62,8 +63,10 @@ def tile_better_transformer_t_v_kernel(
         nc.vector.memset(vec_rows[:], 0.0)
         nc.sync.dma_start(out=vec_rows[0:BLOCKS, :], in_=gamma.rearrange("(r c) -> r c", c=P))
         nc.sync.dma_start(out=vec_rows[BLOCKS : 2 * BLOCKS, :], in_=beta.rearrange("(r c) -> r c", c=P))
-        gain_bf = keep.tile([P, 1], BF16)
-        nc.scalar.dma_start(out=gain_bf[:], in_=gain.partition_broadcast(P))
+        nc.sync.dma_start(out=vec_rows[GAIN_ROW : GAIN_ROW + 1, 0:1], in_=gain.rearrange("(a b) -> a b", b=1))
+        pick_gain = keep.tile([P, P], BF16)
+        nc.vector.memset(pick_gain[:], 0.0)
+        nc.vector.memset(pick_gain[GAIN_ROW : GAIN_ROW + 1, :], 1.0)
 
         w_rows = {}
         y_rows = {}
@@ -111,7 +114,10 @@ def tile_better_transformer_t_v_kernel(
         nc.vector.tensor_scalar(
             out=neg_half_beta_col[:], in0=vec_cols[:, 0, BLOCKS : 2 * BLOCKS], scalar1=-0.5, scalar2=None, op0=ALU.mult
         )
+        gain_spread = psum_dx.tile([P, PART], F32, name="gain_spread", tag="dx")
+        nc.tensor.matmul(out=gain_spread[:, 0:P], lhsT=pick_gain[:], rhs=vec_rows[:], start=True, stop=True)
         gain_col = keep.tile([P, 1], F32)
+        nc.vector.tensor_copy(out=gain_col[:], in_=gain_spread[:, 0:1])
 
         w_grouped = keep.tile([P, PARTS, PART, PACK], BF16, align_bytes=64)
         w_codes = keep.tile([P, PARTS, PART], U32, align_bytes=64)
@@ -306,8 +312,6 @@ def tile_better_transformer_t_v_kernel(
             if k in (2, 3):
                 prepare_weights(2 * (k - 2))
                 prepare_weights(2 * (k - 2) + 1)
-            if k == 3:
-                nc.vector.tensor_copy(out=gain_col[:], in_=gain_bf[:])
             if live(k - 4):
                 add_residual_and_store(k - 4, 1)
 

from contextlib import ExitStack

import concourse.mybir as mybir
from concourse.masks import make_identity

F32 = mybir.dt.float32
BF16 = mybir.dt.bfloat16
U32 = mybir.dt.uint32
U8 = mybir.dt.uint8
E4M3_X4 = mybir.dt.float8_e4m3fn_x4
E5M2_X4 = mybir.dt.float8_e5m2_x4
ACT = mybir.ActivationFunctionType
ALU = mybir.AluOpType

P = 128
PACK = 4
TOKENS = 2048
PARTS = 2
PART = P * PACK
FEATURES = PARTS * PART
BLOCKS = FEATURES // P
TILES = TOKENS // P
GROUP = 4
GROUP_TOKENS = GROUP * P
UNITS = (TILES // GROUP) * PARTS
PAIR = 2
PAIR_TOKENS = PAIR * P
HALVES = UNITS * 2
W_PIECES = 2 * PARTS
GAIN_ROW = 32
EARLY = 3

FLOPS = 2 * TOKENS * PART * PART * PARTS
BYTES = TOKENS * FEATURES * (4 + 2 + 4) + PARTS * PART * PART * 2 + 2 * FEATURES * 2 + 2


def tile_better_transformer_t_v_kernel(
    tc, x, weights, bias, gain, norm_bias, gamma, beta, y, grad_out, out
):
    nc = tc.nc

    y_view = y.rearrange("(p j) f -> p j f", j=TILES)
    g_view = grad_out.rearrange("(p j) f -> p j f", j=TILES)
    out_view = out.rearrange("(p j) f -> p j f", j=TILES)

    def place(u):
        return (u // PARTS) * GROUP, u % PARTS

    with ExitStack() as ctx:
        ctx.enter_context(tc.manual_schedule())
        keep = ctx.enter_context(tc.tile_pool(name="keep", bufs=1))
        work = ctx.enter_context(tc.tile_pool(name="work", bufs=3))
        store = ctx.enter_context(tc.tile_pool(name="store", bufs=2 * GROUP))
        psum_y = ctx.enter_context(tc.psum_pool(name="psum_y", bufs=2 * PAIR))
        psum_g = ctx.enter_context(tc.psum_pool(name="psum_g", bufs=2))
        psum_dx = ctx.enter_context(tc.psum_pool(name="psum_dx", bufs=PAIR))

        warm = keep.tile([P, 1], F32)
        nc.vector.memset(warm[:], 0.0)
        nc.scalar.activation(out=warm[:], in_=warm[:], func=ACT.Silu)

        vec_rows = keep.tile([P, P], BF16)
        nc.vector.memset(vec_rows[:], 0.0)
        nc.sync.dma_start(out=vec_rows[0:BLOCKS, :], in_=gamma.rearrange("(r c) -> r c", c=P))
        nc.sync.dma_start(out=vec_rows[BLOCKS : 2 * BLOCKS, :], in_=beta.rearrange("(r c) -> r c", c=P))
        nc.sync.dma_start(out=vec_rows[GAIN_ROW : GAIN_ROW + 1, 0:1], in_=gain.rearrange("(a b) -> a b", b=1))
        pick_gain = keep.tile([P, P], BF16)
        nc.vector.memset(pick_gain[:], 0.0)
        nc.vector.memset(pick_gain[GAIN_ROW : GAIN_ROW + 1, :], 1.0)

        w_rows = {}
        y_rows = {}
        g_rows = {}
        for u in range(UNITS):
            tile0, q = place(u)
            tiles = slice(tile0, tile0 + GROUP)
            if u < PARTS:
                for half in range(2):
                    first = q * PART + half * PAIR * P
                    y_piece = keep.tile([P, GROUP, PAIR * P], F32, name="y_rows_%d_%d" % (u, half))
                    nc.sync.dma_start(out=y_piece[:], in_=y_view[:, tiles, first : first + PAIR * P])
                    y_rows[2 * u + half] = y_piece[:]
                    if half == u:
                        g_piece = keep.tile([P, GROUP, PART], BF16, name="g_rows_%d" % u)
                        nc.sync.dma_start(out=g_piece[:], in_=g_view[:, tiles, q * PART : (q + 1) * PART])
                        g_rows[u] = g_piece[:]
                w_rows[q] = keep.tile([P, PACK, PART], BF16, name="w_rows_%d" % q)
                nc.sync.dma_start(out=w_rows[q][:], in_=weights[q].rearrange("(a p) o -> p a o", p=P))
            else:
                y_unit = keep.tile([P, GROUP, PART], F32, name="y_rows_%d" % u)
                nc.sync.dma_start(out=y_unit[:], in_=y_view[:, tiles, q * PART : (q + 1) * PART])
                for half in range(2):
                    y_rows[2 * u + half] = y_unit[:, :, half * PAIR * P : (half + 1) * PAIR * P]
                if q == 0:
                    g_group = keep.tile([P, GROUP, FEATURES], BF16, name="g_rows_%d" % u)
                    nc.sync.dma_start(out=g_group[:], in_=g_view[:, tiles, :])
                    for part in range(PARTS):
                        g_rows[u + part] = g_group[:, :, part * PART : (part + 1) * PART]

        ident_f32 = keep.tile([P, P], F32)
        make_identity(nc, ident_f32[:])
        ident_bf = keep.tile([P, P], BF16)
        make_identity(nc, ident_bf[:])

        vec_cols = psum_g.tile([P, PAIR, GROUP_TOKENS], BF16, tag="g_turned")
        nc.tensor.transpose(vec_cols[:, 0, 0:P], vec_rows[:], ident_bf[:])
        c_col = keep.tile([P, BLOCKS], F32)
        nc.vector.tensor_scalar(
            out=c_col[:], in0=vec_cols[:, 0, 0:BLOCKS], scalar1=-0.5, scalar2=0.5, op0=ALU.mult, op1=ALU.add
        )
        beta_col = keep.tile([P, BLOCKS], F32)
        nc.vector.tensor_copy(out=beta_col[:], in_=vec_cols[:, 0, BLOCKS : 2 * BLOCKS])
        neg_half_beta_col = keep.tile([P, BLOCKS], F32)
        nc.vector.tensor_scalar(
            out=neg_half_beta_col[:], in0=vec_cols[:, 0, BLOCKS : 2 * BLOCKS], scalar1=-0.5, scalar2=None, op0=ALU.mult
        )
        gain_spread = psum_dx.tile([P, PART], F32, name="gain_spread", tag="dx")
        nc.tensor.matmul(out=gain_spread[:, 0:P], lhsT=pick_gain[:], rhs=vec_rows[:], start=True, stop=True)
        gain_col = keep.tile([P, 1], F32)
        nc.vector.tensor_copy(out=gain_col[:], in_=gain_spread[:, 0:1])

        w_grouped = keep.tile([P, PARTS, PART, PACK], BF16, align_bytes=64)
        w_codes = keep.tile([P, PARTS, PART], U32, align_bytes=64)
        w_scales = keep.tile([P, PARTS, PART], U8, align_bytes=64)

        def prepare_weights(piece):
            q, half = piece // 2, piece % 2
            w_turned = psum_dx.tile([P, PACK, PAIR_TOKENS], BF16, name="w_turned_%d" % piece, tag="dx")
            for t in range(PACK):
                for s in range(PAIR):
                    nc.tensor.transpose(
                        w_turned[:, t, s * P : (s + 1) * P],
                        w_rows[q][:, half * PAIR + s, t * P : (t + 1) * P],
                        ident_bf[:],
                    )
            nc.vector.tensor_copy(
                out=w_grouped[:, q, half * PAIR_TOKENS : (half + 1) * PAIR_TOKENS, :],
                in_=w_turned[:].rearrange("p t i -> p i t"),
            )
            if half == 1:
                nc.vector.quantize_mx(
                    out=w_codes[:, q, :].bitcast(E4M3_X4),
                    scales=w_scales[:, q, :],
                    in_=w_grouped[:, q].rearrange("p i t -> p (i t)"),
                )

        y_turned = {}
        g_turned = {}
        silu = {}
        c_sig = {}
        product = {}
        dy_pairs = {}
        dy_grouped = {}
        dy_codes = {}
        dy_scales = {}
        dx = {}
        result = {}

        def turn_y(i):
            for s in range(PAIR):
                y_turned[i, s] = psum_y.tile([P, GROUP_TOKENS], F32, name="y_turned_%d_%d" % (i, s), tag="y_turned")
                for j in range(GROUP):
                    nc.tensor.transpose(
                        y_turned[i, s][:, j * P : (j + 1) * P], y_rows[i][:, j, s * P : (s + 1) * P], ident_f32[:]
                    )

        def turn_grad_out(i):
            g_turned[i] = psum_g.tile([P, PAIR, GROUP_TOKENS], BF16, name="g_turned_%d" % i, tag="g_turned")
            for s in range(PAIR):
                first = ((i % 2) * PAIR + s) * P
                for j in range(GROUP):
                    nc.tensor.transpose(
                        g_turned[i][:, s, j * P : (j + 1) * P], g_rows[i // 2][:, j, first : first + P], ident_bf[:]
                    )

        def block_of(i, s):
            return place(i // 2)[1] * PACK + (i % 2) * PAIR + s

        def functions_of_y(i):
            silu[i] = work.tile([P, PAIR, GROUP_TOKENS], F32, name="silu_%d" % i, tag="silu")
            c_sig[i] = work.tile([P, PAIR, GROUP_TOKENS], F32, name="c_sig_%d" % i, tag="c_sig")
            for s in range(PAIR):
                b = block_of(i, s)
                nc.scalar.activation(
                    out=c_sig[i][:, s, :], in_=y_turned[i, s][:], func=ACT.Tanh, scale=neg_half_beta_col[:, b : b + 1]
                )
                nc.scalar.activation(
                    out=silu[i][:, s, :], in_=y_turned[i, s][:], func=ACT.Silu, scale=beta_col[:, b : b + 1]
                )
                if i >= EARLY:
                    nc.scalar.activation(
                        out=c_sig[i][:, s, :],
                        in_=c_sig[i][:, s, :],
                        func=ACT.Identity,
                        scale=c_col[:, b : b + 1],
                        bias=c_col[:, b : b + 1],
                    )

        def scale_tanh_on_vector(i):
            for s in range(PAIR):
                b = block_of(i, s)
                nc.vector.tensor_scalar(
                    out=c_sig[i][:, s, :],
                    in0=c_sig[i][:, s, :],
                    scalar1=c_col[:, b : b + 1],
                    scalar2=c_col[:, b : b + 1],
                    op0=ALU.mult,
                    op1=ALU.add,
                )

        def product_of_functions(i):
            product[i] = work.tile([P, PAIR, GROUP_TOKENS], F32, name="product_%d" % i, tag="product")
            nc.vector.scalar_tensor_tensor(
                out=product[i][:].rearrange("p s r -> p (s r)"),
                in0=silu[i][:].rearrange("p s r -> p (s r)"),
                scalar=1.0,
                in1=c_sig[i][:].rearrange("p s r -> p (s r)"),
                op0=ALU.subtract,
                op1=ALU.mult,
            )

        def gradient_of_y(i):
            u = i // 2
            if i % 2 == 0:
                dy_pairs[u] = work.tile([P, PAIR, GROUP_TOKENS, PAIR], BF16, name="dy_pairs_%d" % u, tag="dy_pairs")
            nc.vector.scalar_tensor_tensor(
                out=dy_pairs[u][:, i % 2, :, :],
                in0=product[i][:].rearrange("p s r -> p r s"),
                scalar=1.0,
                in1=g_turned[i][:].rearrange("p s r -> p r s"),
                op0=ALU.add,
                op1=ALU.mult,
            )

        def merge_pairs(i):
            first = (i % 2) * PAIR_TOKENS
            dy_grouped[i] = work.tile([P, PAIR_TOKENS, PACK], BF16, name="dy_grouped_%d" % i, tag="dy_grouped", align_bytes=64)
            nc.scalar.copy(
                out=dy_grouped[i][:].rearrange("p r t -> p (r t)").bitcast(F32).rearrange("p (r h) -> p r h", h=PAIR),
                in_=dy_pairs[i // 2][:]
                .rearrange("p h r s -> p h (r s)")
                .bitcast(F32)[:, :, first : first + PAIR_TOKENS]
                .rearrange("p h r -> p r h"),
            )

        def quantise(i):
            dy_codes[i] = work.tile([P, PAIR_TOKENS], U32, name="dy_codes_%d" % i, tag="dy_codes", align_bytes=64)
            dy_scales[i] = work.tile([P, PAIR_TOKENS], U8, name="dy_scales_%d" % i, tag="dy_scales", align_bytes=64)
            nc.vector.quantize_mx(
                out=dy_codes[i][:].bitcast(E5M2_X4),
                scales=dy_scales[i][:],
                in_=dy_grouped[i][:].rearrange("p r t -> p (r t)"),
            )

        def multiply(i, banks, tag):
            q = place(i // 2)[1]
            for s in range(PAIR):
                dx[i, s] = banks.tile([P, PART], F32, name="dx_%d_%d" % (i, s), tag=tag)
                nc.tensor.matmul_mx(
                    out=dx[i, s][:],
                    lhsT=dy_codes[i][:, s * P : (s + 1) * P].bitcast(E5M2_X4),
                    lhsT_scale=dy_scales[i][:, s * P : (s + 1) * P],
                    rhs=w_codes[:, q, :].bitcast(E4M3_X4),
                    rhs_scale=w_scales[:, q, :],
                    start=True,
                    stop=True,
                )

        def add_residual_and_store(i, s):
            u = i // 2
            tile0, q = place(u)
            j = (i % 2) * PAIR + s
            if q == 0:
                result[tile0 + j] = store.tile([P, FEATURES], F32, name="result_%d" % (tile0 + j), tag="result")
            nc.vector.scalar_tensor_tensor(
                out=result[tile0 + j][:, q * PART : (q + 1) * PART],
                in0=dx[i, s][:],
                scalar=gain_col[:, 0:1],
                in1=g_rows[u][:, j, :],
                op0=ALU.mult,
                op1=ALU.add,
            )
            if u >= UNITS - PARTS:
                nc.sync.dma_start(
                    out=out_view[:, tile0 + j, q * PART : (q + 1) * PART], in_=result[tile0 + j][:, q * PART : (q + 1) * PART]
                )
            elif q == PARTS - 1:
                nc.sync.dma_start(out=out_view[:, tile0 + j, :], in_=result[tile0 + j][:])

        def live(i):
            return 0 <= i < HALVES

        turn_y(0)
        for k in range(HALVES):
            if live(k + 1):
                turn_y(k + 1)
            turn_grad_out(k)
            functions_of_y(k)
            if live(k - 3):
                merge_pairs(k - 3)
            if live(k - 4):
                quantise(k - 4)
                multiply(k - 4, psum_dx, "dx")
            if live(k - 1):
                product_of_functions(k - 1)
            if k < EARLY:
                scale_tanh_on_vector(k)
            if live(k - 4):
                add_residual_and_store(k - 4, 0)
            if live(k - 1):
                gradient_of_y(k - 1)
            if k in (2, 3):
                prepare_weights(2 * (k - 2))
                prepare_weights(2 * (k - 2) + 1)
            if live(k - 4):
                add_residual_and_store(k - 4, 1)

        last = HALVES - 1
        merge_pairs(last - 2)
        product_of_functions(last)
        quantise(last - 3)
        multiply(last - 3, psum_dx, "dx")
        gradient_of_y(last)
        merge_pairs(last - 1)
        merge_pairs(last)
        quantise(last - 2)
        multiply(last - 2, psum_y, "y_turned")
        add_residual_and_store(last - 3, 0)
        add_residual_and_store(last - 3, 1)
        quantise(last - 1)
        multiply(last - 1, psum_y, "y_turned")
        add_residual_and_store(last - 2, 0)
        add_residual_and_store(last - 2, 1)
        quantise(last)
        multiply(last, psum_dx, "dx")
        add_residual_and_store(last - 1, 0)
        add_residual_and_store(last - 1, 1)
        add_residual_and_store(last, 0)
        add_residual_and_store(last, 1)
